import numpy as np
import ml_dtypes


def mxq(x, axis, fmt="e4m3"):
    dtype, down = {"e4m3": (ml_dtypes.float8_e4m3fn, 7), "e5m2": (ml_dtypes.float8_e5m2, 14)}[fmt]
    v = np.moveaxis(np.asarray(x, np.float32).astype(ml_dtypes.bfloat16).astype(np.float64), axis, -1)
    blocks = v.reshape(v.shape[:-1] + (-1, 32))
    amax = np.abs(blocks).max(-1, keepdims=True)
    byte = np.maximum(np.where(amax > 0, np.frexp(amax)[1] - 1 + 127, 0) - down, 1)
    scale = np.exp2(byte - 127.0)
    codes = (blocks / scale).astype(np.float32).astype(dtype).astype(np.float64)
    return np.moveaxis((codes * scale).reshape(v.shape), -1, axis)


WIDE = False


def mx_kscale(k):
    if not WIDE:
        return np.ones(k)
    levels = np.array([10, -10, 5, -5, 0])
    a = np.random.permutation(np.resize(levels, k // 512 * 4)).reshape(k // 512, 4)
    idx = np.arange(k)
    return np.exp2(a[idx // 512, idx % 128 // 32])


BF16 = ml_dtypes.bfloat16


def bf(x):
    return np.asarray(x, np.float32).astype(BF16)


def f64(x):
    return np.asarray(x).astype(np.float64)


B, D, U, L, G, P, NG = 128, 512, 256, 3, 1, 1, 4
NB = G + P
C = (1 + L) * U


def silu(v):
    return v / (1.0 + np.exp(-v))


def knots():
    return -1.0 + (2.0 / G) * np.arange(-P, G + P + 1)


def bspline_basis(x, grid, k):
    xe = x[..., None]
    b = np.where((xe >= grid[:-1]) & (xe < grid[1:]), 1.0, 0.0)
    for p in range(1, k + 1):
        left = (xe - grid[:-(p + 1)]) / (grid[p:-1] - grid[:-(p + 1)]) * b[..., :-1]
        right = (grid[p + 1:] - xe) / (grid[p + 1:] - grid[1:-p]) * b[..., 1:]
        b = left + right
    return b


def setup_inputs():
    t = mx_kscale(C)
    tk = t[U:].reshape(L, 1, U)
    return {
        "x": bf(np.random.standard_normal((B, D))),
        "lstm_out": bf(np.random.standard_normal((B, U)) * 0.3 * t[:U]),
        "kan_base_w": bf(np.random.standard_normal((L, D, U)) / np.sqrt(D) * tk),
        "kan_spline_w": bf(np.random.standard_normal((L, D * NB, U)) / np.sqrt(D) * tk),
        "combine_w": bf(np.random.standard_normal((C, U)) / np.sqrt(C) / t[:, None]),
        "combine_b": bf(np.random.standard_normal(U) * 0.2),
    }


def reference(x, lstm_out, kan_base_w, kan_spline_w, combine_w, combine_b):
    x = f64(x)
    bases = bspline_basis(x, knots(), P)
    base_out = mxq(silu(x), 1, "e4m3") @ mxq(f64(kan_base_w), 1, "e4m3")
    spline_out = mxq(bases.reshape(B, D * NB), 1, "e4m3") @ mxq(f64(kan_spline_w), 1, "e4m3")
    kan_out = base_out + spline_out
    kan_concat = kan_out.transpose(1, 0, 2).reshape(B, L * U)
    combined = np.concatenate([f64(lstm_out), kan_concat], axis=-1)
    return (mxq(combined, 1, "e4m3") @ mxq(f64(combine_w), 0, "e4m3")) + f64(combine_b)

@@ -1,0 +1,219 @@
+from contextlib import ExitStack
+
+import concourse.mybir as mybir
+from concourse.masks import make_identity
+
+F32 = mybir.dt.float32
+BF16 = mybir.dt.bfloat16
+U32 = mybir.dt.uint32
+U8 = mybir.dt.uint8
+FP8X4 = mybir.dt.float8_e4m3fn_x4
+ACT = mybir.ActivationFunctionType
+ALU = mybir.AluOpType
+
+P = 128
+PACK = 4
+B = 128
+D = 512
+U = 256
+L = 3
+NB = 2
+C = (1 + L) * U
+HALVES = U // P
+
+FLOPS = 2 * B * (L * D * U + L * D * NB * U + C * U)
+
+
+def regroup(copy, grouped, raw):
+    copy(
+        out=grouped.rearrange("p (c i) j -> p c j i", i=4),
+        in_=raw.rearrange("p j (c i) -> p c j i", i=4),
+    )
+
+
+def quantise(nc, codes, scales, grouped):
+    nc.vector.quantize_mx(out=codes.bitcast(FP8X4), scales=scales, in_=grouped)
+
+
+def tile_tkancell_pa_s_kernel(
+    tc, x, lstm_out, kan_base_w, kan_spline_w, combine_w, combine_b, out
+):
+    nc = tc.nc
+    with ExitStack() as ctx:
+        keep = ctx.enter_context(tc.tile_pool(name="keep", bufs=1))
+        psum = ctx.enter_context(tc.psum_pool(name="psum", bufs=1))
+
+        x_sb = keep.tile([B, D], BF16)
+        nc.sync.dma_start(out=x_sb[:], in_=x)
+        lstm_sb = keep.tile([B, U], BF16)
+        nc.sync.dma_start(out=lstm_sb[:], in_=lstm_out)
+        bias_rows = keep.tile([P, U], BF16)
+        nc.vector.memset(bias_rows[:], 0.0)
+        nc.sync.dma_start(out=bias_rows[0:1, :], in_=combine_b.rearrange("(o n) -> o n", o=1))
+        base_raw = []
+        spline_raw = []
+        for l in range(L):
+            base_raw_l = keep.tile([P, PACK, U], BF16, name="base_raw%d" % l)
+            nc.sync.dma_start(
+                out=base_raw_l[:], in_=kan_base_w[l].rearrange("(p j) w -> p j w", j=PACK)
+            )
+            base_raw.append(base_raw_l)
+            spline_raw_l = keep.tile([P, NB, PACK, U], BF16, name="spline_raw%d" % l)
+            nc.sync.dma_start(
+                out=spline_raw_l[:],
+                in_=kan_spline_w[l].rearrange("(p c j) w -> p c j w", c=NB, j=PACK),
+            )
+            spline_raw.append(spline_raw_l)
+        cw_raw = keep.tile([P, 2, PACK, U], BF16)
+        nc.sync.dma_start(
+            out=cw_raw[:], in_=combine_w.rearrange("(g t p) n -> p g t n", g=2, t=PACK)
+        )
+
+        ident_f32 = keep.tile([P, P], F32)
+        make_identity(nc, ident_f32[:])
+        ident_bf16 = keep.tile([P, P], BF16)
+        make_identity(nc, ident_bf16[:])
+        ones = keep.tile([P, P], BF16)
+        nc.vector.memset(ones[:], 1.0)
+        knot_shift = keep.tile([P, NB], F32)
+        nc.vector.memset(knot_shift[:, 0:1], 0.5)
+        nc.vector.memset(knot_shift[:, 1:2], -0.5)
+        one = keep.tile([P, 1], F32)
+        nc.vector.memset(one[:], 1.0)
+
+        xt_ps = psum.tile([P, 2, B], F32)
+        x_words = x_sb[:].bitcast(F32).rearrange("b (p c) -> b c p", c=2)
+        for c in range(2):
+            nc.tensor.transpose(xt_ps[:, c, :], x_words[:, c, :], ident_f32[:])
+        xt = xt_ps[:].rearrange("p c b -> p (c b)").bitcast(BF16)
+
+        silu_grouped = keep.tile([P, B, PACK], BF16, align_bytes=64)
+        nc.scalar.activation(
+            out=silu_grouped[:].rearrange("p b (c e) -> p b c e", c=2),
+            in_=xt.rearrange("p (c b e) -> p b c e", c=2, e=2),
+            func=ACT.Silu,
+        )
+        half_dist = keep.tile([P, NB, 2 * 2 * B], F32)
+        for k in range(NB):
+            nc.scalar.activation(
+                out=half_dist[:, k, :],
+                in_=xt,
+                func=ACT.Abs,
+                scale=0.5,
+                bias=knot_shift[:, k : k + 1],
+            )
+        bases_grouped = keep.tile([P, 2, B, PACK], BF16, align_bytes=64)
+        nc.scalar.activation(
+            out=bases_grouped[:].rearrange("p c b (e k) -> p (c b e) k", k=NB),
+            in_=half_dist[:].rearrange("p k n -> p n k"),
+            func=ACT.Relu,
+            scale=-1.0,
+            bias=one[:],
+        )
+        silu_codes = keep.tile([P, B], U32, align_bytes=64)
+        silu_scales = keep.tile([P, B], U8, align_bytes=64)
+        quantise(nc, silu_codes[:], silu_scales[:], silu_grouped[:].rearrange("p b t -> p (b t)"))
+        bases_codes = keep.tile([P, 2, B], U32, align_bytes=64)
+        bases_scales = keep.tile([P, 2, B], U8, align_bytes=64)
+        quantise(
+            nc,
+            bases_codes[:].rearrange("p c b -> p (c b)"),
+            bases_scales[:].rearrange("p c b -> p (c b)"),
+            bases_grouped[:].rearrange("p c b t -> p (c b t)"),
+        )
+
+        bias_ps = psum.tile([P, U], F32)
+        nc.tensor.matmul(out=bias_ps[:], lhsT=ones[:], rhs=bias_rows[:], start=True, stop=True)
+        bias_all = keep.tile([P, U], F32)
+        nc.vector.tensor_copy(out=bias_all[:], in_=bias_ps[:])
+
+        comb_grouped = [
+            keep.tile([P, B, PACK], BF16, align_bytes=64, name="comb_grouped%d" % g) for g in range(2)
+        ]
+        lstmT_ps = psum.tile([P, HALVES, B], BF16)
+        for h in range(HALVES):
+            nc.tensor.transpose(lstmT_ps[:, h, :], lstm_sb[:, h * P : (h + 1) * P], ident_bf16[:])
+        nc.scalar.copy(
+            out=comb_grouped[0][:, :, 0:HALVES], in_=lstmT_ps[:].rearrange("p h b -> p b h")
+        )
+
+        kan0_ps = psum.tile([P, HALVES, B], F32)
+        kan12_ps = psum.tile([P, 2 * HALVES, B], F32)
+        for l in range(L):
+            base_grouped = keep.tile([P, U, PACK], BF16, align_bytes=64, name="base_grouped%d" % l)
+            regroup(nc.scalar.copy, base_grouped[:], base_raw[l][:])
+            spline_grouped = keep.tile(
+                [P, NB, U, PACK], BF16, align_bytes=64, name="spline_grouped%d" % l
+            )
+            for c in range(NB):
+                regroup(nc.vector.tensor_copy, spline_grouped[:, c, :, :], spline_raw[l][:, c, :, :])
+            base_codes = keep.tile([P, U], U32, align_bytes=64, name="base_codes%d" % l)
+            base_scales = keep.tile([P, U], U8, align_bytes=64, name="base_scales%d" % l)
+            quantise(nc, base_codes[:], base_scales[:], base_grouped[:].rearrange("p w j -> p (w j)"))
+            spline_codes = keep.tile([P, NB, U], U32, align_bytes=64, name="spline_codes%d" % l)
+            spline_scales = keep.tile([P, NB, U], U8, align_bytes=64, name="spline_scales%d" % l)
+            quantise(
+                nc,
+                spline_codes[:].rearrange("p c w -> p (c w)"),
+                spline_scales[:].rearrange("p c w -> p (c w)"),
+                spline_grouped[:].rearrange("p c w j -> p (c w j)"),
+            )
+            for h in range(HALVES):
+                cols = slice(h * P, (h + 1) * P)
+                acc = kan0_ps[:, h, :] if l == 0 else kan12_ps[:, (l - 1) * HALVES + h, :]
+                nc.tensor.matmul_mx(
+                    out=acc,
+                    lhsT=base_codes[:, cols].bitcast(FP8X4),
+                    lhsT_scale=base_scales[:, cols],
+                    rhs=silu_codes[:].bitcast(FP8X4),
+                    rhs_scale=silu_scales[:],
+                    start=True,
+                    stop=False,
+                )
+                for c in range(NB):
+                    nc.tensor.matmul_mx(
+                        out=acc,
+                        lhsT=spline_codes[:, c, cols].bitcast(FP8X4),
+                        lhsT_scale=spline_scales[:, c, cols],
+                        rhs=bases_codes[:, c, :].bitcast(FP8X4),
+                        rhs_scale=bases_scales[:, c, :],
+                        start=False,
+                        stop=(c == NB - 1),
+                    )
+            if l == 0:
+                nc.scalar.copy(
+                    out=comb_grouped[0][:, :, HALVES:PACK],
+                    in_=kan0_ps[:].rearrange("p h b -> p b h"),
+                )
+        nc.scalar.copy(out=comb_grouped[1][:], in_=kan12_ps[:].rearrange("p t b -> p b t"))
+
+        cw_grouped = keep.tile([P, 2, U, PACK], BF16, align_bytes=64)
+        regroup(nc.vector.tensor_copy, cw_grouped[:, 0, :, :], cw_raw[:, 0, :, :])
+        regroup(nc.scalar.copy, cw_grouped[:, 1, :, :], cw_raw[:, 1, :, :])
+        cw_codes = keep.tile([P, 2, U], U32, align_bytes=64)
+        cw_scales = keep.tile([P, 2, U], U8, align_bytes=64)
+        comb_codes = keep.tile([P, 2, B], U32, align_bytes=64)
+        comb_scales = keep.tile([P, 2, B], U8, align_bytes=64)
+        out_ps = psum.tile([B, U], F32)
+        for g in range(2):
+            quantise(
+                nc, cw_codes[:, g, :], cw_scales[:, g, :], cw_grouped[:, g, :, :].rearrange("p w j -> p (w j)")
+            )
+            quantise(
+                nc,
+                comb_codes[:, g, :],
+                comb_scales[:, g, :],
+                comb_grouped[g][:].rearrange("p b t -> p (b t)"),
+            )
+            nc.tensor.matmul_mx(
+                out=out_ps[:],
+                lhsT=comb_codes[:, g, :].bitcast(FP8X4),
+                lhsT_scale=comb_scales[:, g, :],
+                rhs=cw_codes[:, g, :].bitcast(FP8X4),
+                rhs_scale=cw_scales[:, g, :],
+                start=(g == 0),
+                stop=(g == 1),
+            )
+        out_sb = keep.tile([B, U], F32)
+        nc.vector.tensor_tensor(out=out_sb[:], in0=out_ps[:], in1=bias_all[:], op=ALU.add)
+        nc.sync.dma_start(out=out, in_=out_sb[:])

@@ -31,10 +31,6 @@ def regroup(copy, grouped, raw):
     )
 
 
-def quantise(nc, codes, scales, grouped):
-    nc.vector.quantize_mx(out=codes.bitcast(FP8X4), scales=scales, in_=grouped)
-
-
 def tile_tkancell_pa_s_kernel(
     tc, x, lstm_out, kan_base_w, kan_spline_w, combine_w, combine_b, out
 ):
@@ -42,32 +38,59 @@ def tile_tkancell_pa_s_kernel(
     with ExitStack() as ctx:
         keep = ctx.enter_context(tc.tile_pool(name="keep", bufs=1))
         psum = ctx.enter_context(tc.psum_pool(name="psum", bufs=1))
+        ctx.enter_context(tc.manual_schedule())
+
+        def regroup_passes(raws, name):
+            grouped = []
+            for c, raw in enumerate(raws):
+                grouped_c = keep.tile([P, U, PACK], BF16, align_bytes=64, name="%s_grouped%d" % (name, c))
+                regroup(nc.scalar.copy if c == len(raws) - 1 else nc.vector.tensor_copy, grouped_c[:], raw)
+                grouped.append(grouped_c)
+            return grouped
+
+        def quantise(grouped, width, name):
+            codes = keep.tile([P, width], U32, align_bytes=64, name=name + "_codes")
+            scales = keep.tile([P, width], U8, align_bytes=64, name=name + "_scales")
+            nc.vector.quantize_mx(
+                out=codes[:].bitcast(FP8X4), scales=scales[:], in_=grouped.rearrange("p w j -> p (w j)")
+            )
+            return codes, scales
+
+        def mx_pass(acc, stationary, cols, moving, start, stop):
+            nc.tensor.matmul_mx(
+                out=acc,
+                lhsT=stationary[0][:, cols].bitcast(FP8X4),
+                lhsT_scale=stationary[1][:, cols],
+                rhs=moving[0][:].bitcast(FP8X4),
+                rhs_scale=moving[1][:],
+                start=start,
+                stop=stop,
+            )
 
         x_sb = keep.tile([B, D], BF16)
         nc.sync.dma_start(out=x_sb[:], in_=x)
-        lstm_sb = keep.tile([B, U], BF16)
-        nc.sync.dma_start(out=lstm_sb[:], in_=lstm_out)
         bias_rows = keep.tile([P, U], BF16)
         nc.vector.memset(bias_rows[:], 0.0)
         nc.sync.dma_start(out=bias_rows[0:1, :], in_=combine_b.rearrange("(o n) -> o n", o=1))
-        base_raw = []
-        spline_raw = []
+        lstm_sb = keep.tile([B, U], BF16)
+        layer_raw = []
         for l in range(L):
-            base_raw_l = keep.tile([P, PACK, U], BF16, name="base_raw%d" % l)
+            base_raw = keep.tile([P, PACK, U], BF16, name="base_raw%d" % l)
+            nc.sync.dma_start(out=base_raw[:], in_=kan_base_w[l].rearrange("(p j) w -> p j w", j=PACK))
+            spline_raw = keep.tile([P, NB, PACK, U], BF16, name="spline_raw%d" % l)
             nc.sync.dma_start(
-                out=base_raw_l[:], in_=kan_base_w[l].rearrange("(p j) w -> p j w", j=PACK)
+                out=spline_raw[:], in_=kan_spline_w[l].rearrange("(p c j) w -> p c j w", c=NB, j=PACK)
             )
-            base_raw.append(base_raw_l)
-            spline_raw_l = keep.tile([P, NB, PACK, U], BF16, name="spline_raw%d" % l)
+            layer_raw.append([base_raw[:], spline_raw[:, 0, :, :], spline_raw[:, 1, :, :]])
+            if l == 0:
+                nc.sync.dma_start(out=lstm_sb[:], in_=lstm_out)
+        cw_raw = []
+        for g in range(2):
+            cw_raw_g = keep.tile([P, PACK, U], BF16, name="cw_raw%d" % g)
             nc.sync.dma_start(
-                out=spline_raw_l[:],
-                in_=kan_spline_w[l].rearrange("(p c j) w -> p c j w", c=NB, j=PACK),
+                out=cw_raw_g[:], in_=combine_w.rearrange("(g t p) n -> g p t n", g=2, t=PACK)[g]
             )
-            spline_raw.append(spline_raw_l)
-        cw_raw = keep.tile([P, 2, PACK, U], BF16)
-        nc.sync.dma_start(
-            out=cw_raw[:], in_=combine_w.rearrange("(g t p) n -> p g t n", g=2, t=PACK)
-        )
+            cw_raw.append(cw_raw_g[:])
 
         ident_f32 = keep.tile([P, P], F32)
         make_identity(nc, ident_f32[:])
@@ -96,11 +119,7 @@ def tile_tkancell_pa_s_kernel(
         half_dist = keep.tile([P, NB, 2 * 2 * B], F32)
         for k in range(NB):
             nc.scalar.activation(
-                out=half_dist[:, k, :],
-                in_=xt,
-                func=ACT.Abs,
-                scale=0.5,
-                bias=knot_shift[:, k : k + 1],
+                out=half_dist[:, k, :], in_=xt, func=ACT.Abs, scale=0.5, bias=knot_shift[:, k : k + 1]
             )
         bases_grouped = keep.tile([P, 2, B, PACK], BF16, align_bytes=64)
         nc.scalar.activation(
@@ -109,17 +128,6 @@ def tile_tkancell_pa_s_kernel(
             func=ACT.Relu,
             scale=-1.0,
             bias=one[:],
-        )
-        silu_codes = keep.tile([P, B], U32, align_bytes=64)
-        silu_scales = keep.tile([P, B], U8, align_bytes=64)
-        quantise(nc, silu_codes[:], silu_scales[:], silu_grouped[:].rearrange("p b t -> p (b t)"))
-        bases_codes = keep.tile([P, 2, B], U32, align_bytes=64)
-        bases_scales = keep.tile([P, 2, B], U8, align_bytes=64)
-        quantise(
-            nc,
-            bases_codes[:].rearrange("p c b -> p (c b)"),
-            bases_scales[:].rearrange("p c b -> p (c b)"),
-            bases_grouped[:].rearrange("p c b t -> p (c b t)"),
         )
 
         bias_ps = psum.tile([P, U], F32)
@@ -133,87 +141,36 @@ def tile_tkancell_pa_s_kernel(
         lstmT_ps = psum.tile([P, HALVES, B], BF16)
         for h in range(HALVES):
             nc.tensor.transpose(lstmT_ps[:, h, :], lstm_sb[:, h * P : (h + 1) * P], ident_bf16[:])
-        nc.scalar.copy(
-            out=comb_grouped[0][:, :, 0:HALVES], in_=lstmT_ps[:].rearrange("p h b -> p b h")
-        )
+        nc.scalar.copy(out=comb_grouped[0][:, :, 0:HALVES], in_=lstmT_ps[:].rearrange("p h b -> p b h"))
 
+        layer_grouped = [regroup_passes(layer_raw[l], "layer%d" % l) for l in range(2)]
+        acts = [quantise(silu_grouped[:], B, "silu")]
+        for c in range(NB):
+            acts.append(quantise(bases_grouped[:, c, :, :], B, "bases%d" % c))
         kan0_ps = psum.tile([P, HALVES, B], F32)
         kan12_ps = psum.tile([P, 2 * HALVES, B], F32)
         for l in range(L):
-            base_grouped = keep.tile([P, U, PACK], BF16, align_bytes=64, name="base_grouped%d" % l)
-            regroup(nc.scalar.copy, base_grouped[:], base_raw[l][:])
-            spline_grouped = keep.tile(
-                [P, NB, U, PACK], BF16, align_bytes=64, name="spline_grouped%d" % l
-            )
-            for c in range(NB):
-                regroup(nc.vector.tensor_copy, spline_grouped[:, c, :, :], spline_raw[l][:, c, :, :])
-            base_codes = keep.tile([P, U], U32, align_bytes=64, name="base_codes%d" % l)
-            base_scales = keep.tile([P, U], U8, align_bytes=64, name="base_scales%d" % l)
-            quantise(nc, base_codes[:], base_scales[:], base_grouped[:].rearrange("p w j -> p (w j)"))
-            spline_codes = keep.tile([P, NB, U], U32, align_bytes=64, name="spline_codes%d" % l)
-            spline_scales = keep.tile([P, NB, U], U8, align_bytes=64, name="spline_scales%d" % l)
-            quantise(
-                nc,
-                spline_codes[:].rearrange("p c w -> p (c w)"),
-                spline_scales[:].rearrange("p c w -> p (c w)"),
-                spline_grouped[:].rearrange("p c w j -> p (c w j)"),
-            )
+            weights = [
+                quantise(grouped_c[:], U, "layer%d_%d" % (l, c)) for c, grouped_c in enumerate(layer_grouped[l])
+            ]
             for h in range(HALVES):
-                cols = slice(h * P, (h + 1) * P)
                 acc = kan0_ps[:, h, :] if l == 0 else kan12_ps[:, (l - 1) * HALVES + h, :]
-                nc.tensor.matmul_mx(
-                    out=acc,
-                    lhsT=base_codes[:, cols].bitcast(FP8X4),
-                    lhsT_scale=base_scales[:, cols],
-                    rhs=silu_codes[:].bitcast(FP8X4),
-                    rhs_scale=silu_scales[:],
-                    start=True,
-                    stop=False,
-                )
-                for c in range(NB):
-                    nc.tensor.matmul_mx(
-                        out=acc,
-                        lhsT=spline_codes[:, c, cols].bitcast(FP8X4),
-                        lhsT_scale=spline_scales[:, c, cols],
-                        rhs=bases_codes[:, c, :].bitcast(FP8X4),
-                        rhs_scale=bases_scales[:, c, :],
-                        start=False,
-                        stop=(c == NB - 1),
-                    )
+                for c in range(1 + NB):
+                    mx_pass(acc, weights[c], slice(h * P, (h + 1) * P), acts[c], c == 0, c == NB)
+            if l + 2 < L:
+                layer_grouped.append(regroup_passes(layer_raw[l + 2], "layer%d" % (l + 2)))
             if l == 0:
                 nc.scalar.copy(
-                    out=comb_grouped[0][:, :, HALVES:PACK],
-                    in_=kan0_ps[:].rearrange("p h b -> p b h"),
+                    out=comb_grouped[0][:, :, HALVES:PACK], in_=kan0_ps[:].rearrange("p h b -> p b h")
                 )
-        nc.scalar.copy(out=comb_grouped[1][:], in_=kan12_ps[:].rearrange("p t b -> p b t"))
 
-        cw_grouped = keep.tile([P, 2, U, PACK], BF16, align_bytes=64)
-        regroup(nc.vector.tensor_copy, cw_grouped[:, 0, :, :], cw_raw[:, 0, :, :])
-        regroup(nc.scalar.copy, cw_grouped[:, 1, :, :], cw_raw[:, 1, :, :])
-        cw_codes = keep.tile([P, 2, U], U32, align_bytes=64)
-        cw_scales = keep.tile([P, 2, U], U8, align_bytes=64)
-        comb_codes = keep.tile([P, 2, B], U32, align_bytes=64)
-        comb_scales = keep.tile([P, 2, B], U8, align_bytes=64)
+        cw_grouped = regroup_passes(cw_raw, "cw")
+        nc.scalar.copy(out=comb_grouped[1][:], in_=kan12_ps[:].rearrange("p t b -> p b t"))
+        cw = [quantise(cw_grouped[g][:], U, "cw%d" % g) for g in range(2)]
         out_ps = psum.tile([B, U], F32)
         for g in range(2):
-            quantise(
-                nc, cw_codes[:, g, :], cw_scales[:, g, :], cw_grouped[:, g, :, :].rearrange("p w j -> p (w j)")
-            )
-            quantise(
-                nc,
-                comb_codes[:, g, :],
-                comb_scales[:, g, :],
-                comb_grouped[g][:].rearrange("p b t -> p (b t)"),
-            )
-            nc.tensor.matmul_mx(
-                out=out_ps[:],
-                lhsT=comb_codes[:, g, :].bitcast(FP8X4),
-                lhsT_scale=comb_scales[:, g, :],
-                rhs=cw_codes[:, g, :].bitcast(FP8X4),
-                rhs_scale=cw_scales[:, g, :],
-                start=(g == 0),
-                stop=(g == 1),
-            )
+            comb = quantise(comb_grouped[g][:], B, "comb%d" % g)
+            mx_pass(out_ps[:], comb, slice(0, B), cw[g], g == 0, g == 1)
         out_sb = keep.tile([B, U], F32)
         nc.vector.tensor_tensor(out=out_sb[:], in0=out_ps[:], in1=bias_all[:], op=ALU.add)
         nc.sync.dma_start(out=out, in_=out_sb[:])

@@ -20,15 +20,11 @@ L = 3
 NB = 2
 C = (1 + L) * U
 HALVES = U // P
+LAYER_PASSES = 1 + NB
+COMBINE_PASSES = C // (P * PACK)
+SCALAR_FROM = 4
 
 FLOPS = 2 * B * (L * D * U + L * D * NB * U + C * U)
-
-
-def regroup(copy, grouped, raw):
-    copy(
-        out=grouped.rearrange("p (c i) j -> p c j i", i=4),
-        in_=raw.rearrange("p j (c i) -> p c j i", i=4),
-    )
 
 
 def tile_tkancell_pa_s_kernel(
@@ -39,14 +35,6 @@ def tile_tkancell_pa_s_kernel(
         keep = ctx.enter_context(tc.tile_pool(name="keep", bufs=1))
         psum = ctx.enter_context(tc.psum_pool(name="psum", bufs=1))
         ctx.enter_context(tc.manual_schedule())
-
-        def regroup_passes(raws, name):
-            grouped = []
-            for c, raw in enumerate(raws):
-                grouped_c = keep.tile([P, U, PACK], BF16, align_bytes=64, name="%s_grouped%d" % (name, c))
-                regroup(nc.scalar.copy if c == len(raws) - 1 else nc.vector.tensor_copy, grouped_c[:], raw)
-                grouped.append(grouped_c)
-            return grouped
 
         def quantise(grouped, width, name):
             codes = keep.tile([P, width], U32, align_bytes=64, name=name + "_codes")
@@ -67,30 +55,36 @@ def tile_tkancell_pa_s_kernel(
                 stop=stop,
             )
 
+        weight_rows = []
+        for l in range(L):
+            weight_rows.append(kan_base_w[l].rearrange("(p j) w -> p j w", j=PACK))
+            for c in range(NB):
+                weight_rows.append(kan_spline_w[l].rearrange("(p c j) w -> c p j w", c=NB, j=PACK)[c])
+        for g in range(COMBINE_PASSES):
+            weight_rows.append(combine_w.rearrange("(g t p) n -> g p t n", g=COMBINE_PASSES, t=PACK)[g])
+
         x_sb = keep.tile([B, D], BF16)
         nc.sync.dma_start(out=x_sb[:], in_=x)
+        lstm_sb = keep.tile([B, U], BF16)
         bias_rows = keep.tile([P, U], BF16)
         nc.vector.memset(bias_rows[:], 0.0)
-        nc.sync.dma_start(out=bias_rows[0:1, :], in_=combine_b.rearrange("(o n) -> o n", o=1))
-        lstm_sb = keep.tile([B, U], BF16)
-        layer_raw = []
-        for l in range(L):
-            base_raw = keep.tile([P, PACK, U], BF16, name="base_raw%d" % l)
-            nc.sync.dma_start(out=base_raw[:], in_=kan_base_w[l].rearrange("(p j) w -> p j w", j=PACK))
-            spline_raw = keep.tile([P, NB, PACK, U], BF16, name="spline_raw%d" % l)
-            nc.sync.dma_start(
-                out=spline_raw[:], in_=kan_spline_w[l].rearrange("(p c j) w -> p c j w", c=NB, j=PACK)
-            )
-            layer_raw.append([base_raw[:], spline_raw[:, 0, :, :], spline_raw[:, 1, :, :]])
-            if l == 0:
+        weight_raw = []
+        for i, rows in enumerate(weight_rows):
+            if i == LAYER_PASSES:
                 nc.sync.dma_start(out=lstm_sb[:], in_=lstm_out)
-        cw_raw = []
-        for g in range(2):
-            cw_raw_g = keep.tile([P, PACK, U], BF16, name="cw_raw%d" % g)
-            nc.sync.dma_start(
-                out=cw_raw_g[:], in_=combine_w.rearrange("(g t p) n -> g p t n", g=2, t=PACK)[g]
+                nc.sync.dma_start(out=bias_rows[0:1, :], in_=combine_b.rearrange("(o n) -> o n", o=1))
+            raw = keep.tile([P, PACK, U], BF16, name="weight_raw%d" % i)
+            nc.sync.dma_start(out=raw[:], in_=rows)
+            weight_raw.append(raw)
+
+        def regroup(i):
+            grouped = keep.tile([P, U, PACK], BF16, align_bytes=64, name="weight_grouped%d" % i)
+            copy = nc.scalar.copy if i >= SCALAR_FROM and i % 2 == 0 else nc.vector.tensor_copy
+            copy(
+                out=grouped[:].rearrange("p (c i) j -> p c j i", i=4),
+                in_=weight_raw[i][:].rearrange("p j (c i) -> p c j i", i=4),
             )
-            cw_raw.append(cw_raw_g[:])
+            return grouped
 
         ident_f32 = keep.tile([P, P], F32)
         make_identity(nc, ident_f32[:])
@@ -121,7 +115,7 @@ def tile_tkancell_pa_s_kernel(
             nc.scalar.activation(
                 out=half_dist[:, k, :], in_=xt, func=ACT.Abs, scale=0.5, bias=knot_shift[:, k : k + 1]
             )
-        bases_grouped = keep.tile([P, 2, B, PACK], BF16, align_bytes=64)
+        bases_grouped = keep.tile([P, NB, B, PACK], BF16, align_bytes=64)
         nc.scalar.activation(
             out=bases_grouped[:].rearrange("p c b (e k) -> p (c b e) k", k=NB),
             in_=half_dist[:].rearrange("p k n -> p n k"),
@@ -130,47 +124,45 @@ def tile_tkancell_pa_s_kernel(
             bias=one[:],
         )
 
-        bias_ps = psum.tile([P, U], F32)
-        nc.tensor.matmul(out=bias_ps[:], lhsT=ones[:], rhs=bias_rows[:], start=True, stop=True)
-        bias_all = keep.tile([P, U], F32)
-        nc.vector.tensor_copy(out=bias_all[:], in_=bias_ps[:])
-
         comb_grouped = [
-            keep.tile([P, B, PACK], BF16, align_bytes=64, name="comb_grouped%d" % g) for g in range(2)
+            keep.tile([P, B, PACK], BF16, align_bytes=64, name="comb_grouped%d" % g)
+            for g in range(COMBINE_PASSES)
         ]
         lstmT_ps = psum.tile([P, HALVES, B], BF16)
         for h in range(HALVES):
             nc.tensor.transpose(lstmT_ps[:, h, :], lstm_sb[:, h * P : (h + 1) * P], ident_bf16[:])
         nc.scalar.copy(out=comb_grouped[0][:, :, 0:HALVES], in_=lstmT_ps[:].rearrange("p h b -> p b h"))
 
-        layer_grouped = [regroup_passes(layer_raw[l], "layer%d" % l) for l in range(2)]
-        acts = [quantise(silu_grouped[:], B, "silu")]
-        for c in range(NB):
-            acts.append(quantise(bases_grouped[:, c, :, :], B, "bases%d" % c))
+        bias_ps = psum.tile([P, U], F32)
+        nc.tensor.matmul(out=bias_ps[:], lhsT=ones[:], rhs=bias_rows[:], start=True, stop=True)
+
         kan0_ps = psum.tile([P, HALVES, B], F32)
         kan12_ps = psum.tile([P, 2 * HALVES, B], F32)
+        acts = []
         for l in range(L):
-            weights = [
-                quantise(grouped_c[:], U, "layer%d_%d" % (l, c)) for c, grouped_c in enumerate(layer_grouped[l])
-            ]
+            tiles = range(l * LAYER_PASSES, (l + 1) * LAYER_PASSES)
+            grouped = [regroup(i) for i in tiles]
+            weights = [quantise(grouped[c][:], U, "weight%d" % i) for c, i in enumerate(tiles)]
+            if l == 0:
+                acts.append(quantise(silu_grouped[:], B, "silu"))
+                for c in range(NB):
+                    acts.append(quantise(bases_grouped[:, c, :, :], B, "bases%d" % c))
             for h in range(HALVES):
                 acc = kan0_ps[:, h, :] if l == 0 else kan12_ps[:, (l - 1) * HALVES + h, :]
-                for c in range(1 + NB):
+                for c in range(LAYER_PASSES):
                     mx_pass(acc, weights[c], slice(h * P, (h + 1) * P), acts[c], c == 0, c == NB)
-            if l + 2 < L:
-                layer_grouped.append(regroup_passes(layer_raw[l + 2], "layer%d" % (l + 2)))
-            if l == 0:
-                nc.scalar.copy(
-                    out=comb_grouped[0][:, :, HALVES:PACK], in_=kan0_ps[:].rearrange("p h b -> p b h")
-                )
 
-        cw_grouped = regroup_passes(cw_raw, "cw")
+        tiles = range(L * LAYER_PASSES, L * LAYER_PASSES + COMBINE_PASSES)
+        grouped = [regroup(i) for i in tiles]
+        nc.scalar.copy(out=comb_grouped[0][:, :, HALVES:PACK], in_=kan0_ps[:].rearrange("p h b -> p b h"))
         nc.scalar.copy(out=comb_grouped[1][:], in_=kan12_ps[:].rearrange("p t b -> p b t"))
-        cw = [quantise(cw_grouped[g][:], U, "cw%d" % g) for g in range(2)]
+        bias_all = keep.tile([P, U], F32)
+        nc.scalar.copy(out=bias_all[:], in_=bias_ps[:])
+        weights = [quantise(grouped[g][:], U, "weight%d" % i) for g, i in enumerate(tiles)]
         out_ps = psum.tile([B, U], F32)
-        for g in range(2):
+        for g in range(COMBINE_PASSES):
             comb = quantise(comb_grouped[g][:], B, "comb%d" % g)
-            mx_pass(out_ps[:], comb, slice(0, B), cw[g], g == 0, g == 1)
+            mx_pass(out_ps[:], comb, slice(0, B), weights[g], g == 0, g == COMBINE_PASSES - 1)
         out_sb = keep.tile([B, U], F32)
         nc.vector.tensor_tensor(out=out_sb[:], in0=out_ps[:], in1=bias_all[:], op=ALU.add)
         nc.sync.dma_start(out=out, in_=out_sb[:])

@@ -153,8 +153,8 @@ def tile_tkancell_pa_s_kernel(
                     mx_pass(acc, weights[c], slice(h * P, (h + 1) * P), acts[c], c == 0, c == NB)
 
         tiles = range(L * LAYER_PASSES, L * LAYER_PASSES + COMBINE_PASSES)
-        grouped = [regroup(i) for i in tiles]
         nc.scalar.copy(out=comb_grouped[0][:, :, HALVES:PACK], in_=kan0_ps[:].rearrange("p h b -> p b h"))
+        grouped = [regroup(i) for i in tiles]
         nc.scalar.copy(out=comb_grouped[1][:], in_=kan12_ps[:].rearrange("p t b -> p b t"))
         bias_all = keep.tile([P, U], F32)
         nc.scalar.copy(out=bias_all[:], in_=bias_ps[:])

@@ -22,7 +22,7 @@ C = (1 + L) * U
 HALVES = U // P
 LAYER_PASSES = 1 + NB
 COMBINE_PASSES = C // (P * PACK)
-SCALAR_FROM = 4
+BASE0_VECTOR_COLS = 160
 
 FLOPS = 2 * B * (L * D * U + L * D * NB * U + C * U)
 
@@ -39,70 +39,109 @@ def tile_tkancell_pa_s_kernel(
         def quantise(grouped, width, name):
             codes = keep.tile([P, width], U32, align_bytes=64, name=name + "_codes")
             scales = keep.tile([P, width], U8, align_bytes=64, name=name + "_scales")
-            nc.vector.quantize_mx(
-                out=codes[:].bitcast(FP8X4), scales=scales[:], in_=grouped.rearrange("p w j -> p (w j)")
-            )
+            nc.vector.quantize_mx(out=codes[:].bitcast(FP8X4), scales=scales[:], in_=grouped)
             return codes, scales
 
-        def mx_pass(acc, stationary, cols, moving, start, stop):
+        def mx_pass(acc, stationary, cols, moving, moving_cols, start, stop):
             nc.tensor.matmul_mx(
                 out=acc,
                 lhsT=stationary[0][:, cols].bitcast(FP8X4),
                 lhsT_scale=stationary[1][:, cols],
-                rhs=moving[0][:].bitcast(FP8X4),
-                rhs_scale=moving[1][:],
+                rhs=moving[0][:, moving_cols].bitcast(FP8X4),
+                rhs_scale=moving[1][:, moving_cols],
                 start=start,
                 stop=stop,
             )
 
-        weight_rows = []
-        for l in range(L):
-            weight_rows.append(kan_base_w[l].rearrange("(p j) w -> p j w", j=PACK))
-            for c in range(NB):
-                weight_rows.append(kan_spline_w[l].rearrange("(p c j) w -> c p j w", c=NB, j=PACK)[c])
-        for g in range(COMBINE_PASSES):
-            weight_rows.append(combine_w.rearrange("(g t p) n -> g p t n", g=COMBINE_PASSES, t=PACK)[g])
+        one = keep.tile([P, 1], F32)
+        nc.vector.memset(one[:], 1.0)
+        silu_one = keep.tile([P, 1], F32)
+        nc.scalar.activation(out=silu_one[:], in_=one[:], func=ACT.Silu)
 
+        base_raw = []
+        spline_raw = []
         x_sb = keep.tile([B, D], BF16)
-        nc.sync.dma_start(out=x_sb[:], in_=x)
-        lstm_sb = keep.tile([B, U], BF16)
-        bias_rows = keep.tile([P, U], BF16)
-        nc.vector.memset(bias_rows[:], 0.0)
-        weight_raw = []
-        for i, rows in enumerate(weight_rows):
-            if i == LAYER_PASSES:
+        for l in range(L):
+            raw = keep.tile([P, PACK, U], BF16, name="base_raw%d" % l)
+            nc.sync.dma_start(out=raw[:], in_=kan_base_w[l].rearrange("(p j) w -> p j w", j=PACK))
+            base_raw.append(raw)
+            if l == 0:
+                nc.sync.dma_start(out=x_sb[:], in_=x)
+            rows = kan_spline_w[l].rearrange("(p c j) w -> p c j w", c=NB, j=PACK)
+            if l == 0:
+                halves = [keep.tile([P, PACK, U], BF16, name="spline_raw0_%d" % c) for c in range(NB)]
+                for c in range(NB):
+                    nc.sync.dma_start(out=halves[c][:], in_=rows[:, c, :, :])
+                spline_raw.append([half[:] for half in halves])
+                lstm_sb = keep.tile([B, U], BF16)
                 nc.sync.dma_start(out=lstm_sb[:], in_=lstm_out)
-                nc.sync.dma_start(out=bias_rows[0:1, :], in_=combine_b.rearrange("(o n) -> o n", o=1))
-            raw = keep.tile([P, PACK, U], BF16, name="weight_raw%d" % i)
-            nc.sync.dma_start(out=raw[:], in_=rows)
-            weight_raw.append(raw)
-
-        def regroup(i):
-            grouped = keep.tile([P, U, PACK], BF16, align_bytes=64, name="weight_grouped%d" % i)
-            copy = nc.scalar.copy if i >= SCALAR_FROM and i % 2 == 0 else nc.vector.tensor_copy
-            copy(
-                out=grouped[:].rearrange("p (c i) j -> p c j i", i=4),
-                in_=weight_raw[i][:].rearrange("p j (c i) -> p c j i", i=4),
+            else:
+                raw = keep.tile([P, NB, PACK, U], BF16, name="spline_raw%d" % l)
+                nc.sync.dma_start(out=raw[:], in_=rows)
+                spline_raw.append([raw[:, c, :, :] for c in range(NB)])
+        combine_raw = []
+        for g in range(COMBINE_PASSES):
+            raw = keep.tile([P, PACK, U], BF16, name="combine_raw%d" % g)
+            nc.sync.dma_start(
+                out=raw[:], in_=combine_w.rearrange("(g t p) n -> g p t n", g=COMBINE_PASSES, t=PACK)[g]
             )
-            return grouped
+            combine_raw.append(raw)
+        bias_all = keep.tile([P, U], BF16)
+        nc.sync.dma_start(out=bias_all[:], in_=combine_b.partition_broadcast(P))
+
+        def regroup(copy, grouped, raw, lo=0, hi=U):
+            copy(
+                out=grouped[:, lo:hi, :].rearrange("p (c i) j -> p c j i", i=4),
+                in_=raw[:, :, lo:hi].rearrange("p j (c i) -> p c j i", i=4),
+            )
+
+        on_vector = nc.vector.tensor_copy
+        on_scalar = nc.scalar.copy
 
         ident_f32 = keep.tile([P, P], F32)
         make_identity(nc, ident_f32[:])
         ident_bf16 = keep.tile([P, P], BF16)
         make_identity(nc, ident_bf16[:])
-        ones = keep.tile([P, P], BF16)
-        nc.vector.memset(ones[:], 1.0)
         knot_shift = keep.tile([P, NB], F32)
         nc.vector.memset(knot_shift[:, 0:1], 0.5)
         nc.vector.memset(knot_shift[:, 1:2], -0.5)
-        one = keep.tile([P, 1], F32)
-        nc.vector.memset(one[:], 1.0)
 
         xt_ps = psum.tile([P, 2, B], F32)
         x_words = x_sb[:].bitcast(F32).rearrange("b (p c) -> b c p", c=2)
         for c in range(2):
             nc.tensor.transpose(xt_ps[:, c, :], x_words[:, c, :], ident_f32[:])
         xt = xt_ps[:].rearrange("p c b -> p (c b)").bitcast(BF16)
+
+        comb_ps = [psum.tile([P, PACK, B], F32, name="comb_ps%d" % g) for g in range(COMBINE_PASSES)]
+        for h in range(HALVES):
+            nc.tensor.matmul(
+                out=comb_ps[0][:, h, :], lhsT=lstm_sb[:, h * P : (h + 1) * P], rhs=ident_bf16[:], start=True, stop=True
+            )
+        comb_grouped = [
+            keep.tile([P, B, PACK], BF16, align_bytes=64, name="comb_grouped%d" % g)
+            for g in range(COMBINE_PASSES)
+        ]
+
+        layer_grouped = [
+            keep.tile([P, LAYER_PASSES, U, PACK], BF16, align_bytes=64, name="layer_grouped%d" % l)
+            for l in range(L)
+        ]
+        combine_grouped = [
+            keep.tile([P, U, PACK], BF16, align_bytes=64, name="combine_grouped%d" % g)
+            for g in range(COMBINE_PASSES)
+        ]
+
+        def regroup_base(copy, l, lo=0, hi=U):
+            regroup(copy, layer_grouped[l][:, 0, :, :], base_raw[l][:], lo, hi)
+
+        def regroup_spline(copy, l, c):
+            regroup(copy, layer_grouped[l][:, 1 + c, :, :], spline_raw[l][c])
+
+        def regroup_combine(copy, g):
+            regroup(copy, combine_grouped[g][:], combine_raw[g][:])
+
+        regroup_base(on_vector, 0, 0, BASE0_VECTOR_COLS)
+        regroup_base(on_scalar, 0, BASE0_VECTOR_COLS, U)
 
         silu_grouped = keep.tile([P, B, PACK], BF16, align_bytes=64)
         nc.scalar.activation(
@@ -124,45 +163,61 @@ def tile_tkancell_pa_s_kernel(
             bias=one[:],
         )
 
-        comb_grouped = [
-            keep.tile([P, B, PACK], BF16, align_bytes=64, name="comb_grouped%d" % g)
-            for g in range(COMBINE_PASSES)
-        ]
-        lstmT_ps = psum.tile([P, HALVES, B], BF16)
-        for h in range(HALVES):
-            nc.tensor.transpose(lstmT_ps[:, h, :], lstm_sb[:, h * P : (h + 1) * P], ident_bf16[:])
-        nc.scalar.copy(out=comb_grouped[0][:, :, 0:HALVES], in_=lstmT_ps[:].rearrange("p h b -> p b h"))
+        def quantise_slots(l, lo, hi, name):
+            return quantise(layer_grouped[l][:, lo:hi, :, :].rearrange("p s w j -> p (s w j)"), (hi - lo) * U, name)
 
-        bias_ps = psum.tile([P, U], F32)
-        nc.tensor.matmul(out=bias_ps[:], lhsT=ones[:], rhs=bias_rows[:], start=True, stop=True)
-
-        kan0_ps = psum.tile([P, HALVES, B], F32)
-        kan12_ps = psum.tile([P, 2 * HALVES, B], F32)
-        acts = []
-        for l in range(L):
-            tiles = range(l * LAYER_PASSES, (l + 1) * LAYER_PASSES)
-            grouped = [regroup(i) for i in tiles]
-            weights = [quantise(grouped[c][:], U, "weight%d" % i) for c, i in enumerate(tiles)]
-            if l == 0:
-                acts.append(quantise(silu_grouped[:], B, "silu"))
-                for c in range(NB):
-                    acts.append(quantise(bases_grouped[:, c, :, :], B, "bases%d" % c))
+        def layer_matmuls(l, weights):
             for h in range(HALVES):
-                acc = kan0_ps[:, h, :] if l == 0 else kan12_ps[:, (l - 1) * HALVES + h, :]
+                t = (1 + l) * HALVES + h
+                acc = comb_ps[t // PACK][:, t % PACK, :]
                 for c in range(LAYER_PASSES):
-                    mx_pass(acc, weights[c], slice(h * P, (h + 1) * P), acts[c], c == 0, c == NB)
+                    pair, first = weights[c]
+                    act, act_first = acts[c]
+                    mx_pass(
+                        acc,
+                        pair,
+                        slice(first + h * P, first + (h + 1) * P),
+                        act,
+                        slice(act_first, act_first + B),
+                        c == 0,
+                        c == NB,
+                    )
 
-        tiles = range(L * LAYER_PASSES, L * LAYER_PASSES + COMBINE_PASSES)
-        nc.scalar.copy(out=comb_grouped[0][:, :, HALVES:PACK], in_=kan0_ps[:].rearrange("p h b -> p b h"))
-        grouped = [regroup(i) for i in tiles]
-        nc.scalar.copy(out=comb_grouped[1][:], in_=kan12_ps[:].rearrange("p t b -> p b t"))
-        bias_all = keep.tile([P, U], F32)
-        nc.scalar.copy(out=bias_all[:], in_=bias_ps[:])
-        weights = [quantise(grouped[g][:], U, "weight%d" % i) for g, i in enumerate(tiles)]
+        def comb_copy(g):
+            nc.scalar.copy(out=comb_grouped[g][:], in_=comb_ps[g][:].rearrange("p t b -> p b t"))
+
+        regroup_spline(on_vector, 0, 0)
+        base0 = quantise_slots(0, 0, 1, "base0")
+        regroup_spline(on_vector, 0, 1)
+        spline0a = quantise_slots(0, 1, 2, "spline0a")
+        regroup_base(on_vector, 1)
+        silu = quantise(silu_grouped[:].rearrange("p b j -> p (b j)"), B, "silu")
+        spline0b = quantise_slots(0, 2, 3, "spline0b")
+        base1 = quantise_slots(1, 0, 1, "base1")
+        regroup_spline(on_scalar, 1, 0)
+        regroup_spline(on_scalar, 1, 1)
+        regroup_base(on_vector, 2)
+        bases = quantise(bases_grouped[:].rearrange("p c b j -> p (c b j)"), NB * B, "bases")
+        acts = [(silu, 0), (bases, 0), (bases, B)]
+        layer_matmuls(0, [(base0, 0), (spline0a, 0), (spline0b, 0)])
+        regroup_spline(on_vector, 2, 0)
+        regroup_spline(on_scalar, 2, 1)
+        spline1 = quantise_slots(1, 1, 3, "spline1")
+        layer_matmuls(1, [(base1, 0), (spline1, 0), (spline1, U)])
+        comb_copy(0)
+        base2 = quantise_slots(2, 0, 2, "base2")
+        spline2 = quantise_slots(2, 2, 3, "spline2")
+        layer_matmuls(2, [(base2, 0), (base2, U), (spline2, 0)])
+        regroup_combine(on_vector, 0)
+        regroup_combine(on_scalar, 1)
+        comb_copy(1)
+        comb0 = quantise(comb_grouped[0][:].rearrange("p b j -> p (b j)"), B, "comb0")
+        combine0 = quantise(combine_grouped[0][:].rearrange("p w j -> p (w j)"), U, "combine0")
         out_ps = psum.tile([B, U], F32)
-        for g in range(COMBINE_PASSES):
-            comb = quantise(comb_grouped[g][:], B, "comb%d" % g)
-            mx_pass(out_ps[:], comb, slice(0, B), weights[g], g == 0, g == COMBINE_PASSES - 1)
+        mx_pass(out_ps[:], comb0, slice(0, B), combine0, slice(0, U), True, False)
+        combine1 = quantise(combine_grouped[1][:].rearrange("p w j -> p (w j)"), U, "combine1")
+        comb1 = quantise(comb_grouped[1][:].rearrange("p b j -> p (b j)"), B, "comb1")
+        mx_pass(out_ps[:], comb1, slice(0, B), combine1, slice(0, U), False, True)
         out_sb = keep.tile([B, U], F32)
         nc.vector.tensor_tensor(out=out_sb[:], in0=out_ps[:], in1=bias_all[:], op=ALU.add)
         nc.sync.dma_start(out=out, in_=out_sb[:])

@@ -22,7 +22,6 @@ C = (1 + L) * U
 HALVES = U // P
 LAYER_PASSES = 1 + NB
 COMBINE_PASSES = C // (P * PACK)
-BASE0_VECTOR_COLS = 160
 
 FLOPS = 2 * B * (L * D * U + L * D * NB * U + C * U)
 
@@ -61,38 +60,45 @@ def tile_tkancell_pa_s_kernel(
         base_raw = []
         spline_raw = []
         x_sb = keep.tile([B, D], BF16)
+        nc.sync.dma_start(out=x_sb[:], in_=x)
         for l in range(L):
             raw = keep.tile([P, PACK, U], BF16, name="base_raw%d" % l)
             nc.sync.dma_start(out=raw[:], in_=kan_base_w[l].rearrange("(p j) w -> p j w", j=PACK))
             base_raw.append(raw)
-            if l == 0:
-                nc.sync.dma_start(out=x_sb[:], in_=x)
             rows = kan_spline_w[l].rearrange("(p c j) w -> p c j w", c=NB, j=PACK)
             if l == 0:
                 halves = [keep.tile([P, PACK, U], BF16, name="spline_raw0_%d" % c) for c in range(NB)]
                 for c in range(NB):
                     nc.sync.dma_start(out=halves[c][:], in_=rows[:, c, :, :])
                 spline_raw.append([half[:] for half in halves])
-                lstm_sb = keep.tile([B, U], BF16)
-                nc.sync.dma_start(out=lstm_sb[:], in_=lstm_out)
             else:
                 raw = keep.tile([P, NB, PACK, U], BF16, name="spline_raw%d" % l)
                 nc.sync.dma_start(out=raw[:], in_=rows)
                 spline_raw.append([raw[:, c, :, :] for c in range(NB)])
+            if l == 1:
+                lstm_sb = keep.tile([B, U], BF16)
+                nc.sync.dma_start(out=lstm_sb[:], in_=lstm_out)
         combine_raw = []
         for g in range(COMBINE_PASSES):
             raw = keep.tile([P, PACK, U], BF16, name="combine_raw%d" % g)
             nc.sync.dma_start(
-                out=raw[:], in_=combine_w.rearrange("(g t p) n -> g p t n", g=COMBINE_PASSES, t=PACK)[g]
+                out=raw[:].rearrange("p (s e) n -> p s e n", s=2),
+                in_=combine_w.rearrange("(g s p e) n -> g p s e n", g=COMBINE_PASSES, s=2, e=2)[g],
             )
             combine_raw.append(raw)
         bias_all = keep.tile([P, U], BF16)
         nc.sync.dma_start(out=bias_all[:], in_=combine_b.partition_broadcast(P))
 
-        def regroup(copy, grouped, raw, lo=0, hi=U):
+        def regroup(copy, grouped, raw):
             copy(
-                out=grouped[:, lo:hi, :].rearrange("p (c i) j -> p c j i", i=4),
-                in_=raw[:, :, lo:hi].rearrange("p j (c i) -> p c j i", i=4),
+                out=grouped.rearrange("p (c i) j -> p c j i", i=4),
+                in_=raw.rearrange("p j (c i) -> p c j i", i=4),
+            )
+
+        def regroup_kan(copy, grouped, raw):
+            copy(
+                out=grouped.rearrange("p (e c a) j -> p c j a e", e=2, a=2),
+                in_=raw.rearrange("p j (c a e) -> p c j a e", a=2, e=2),
             )
 
         on_vector = nc.vector.tensor_copy
@@ -113,10 +119,9 @@ def tile_tkancell_pa_s_kernel(
         xt = xt_ps[:].rearrange("p c b -> p (c b)").bitcast(BF16)
 
         comb_ps = [psum.tile([P, PACK, B], F32, name="comb_ps%d" % g) for g in range(COMBINE_PASSES)]
-        for h in range(HALVES):
-            nc.tensor.matmul(
-                out=comb_ps[0][:, h, :], lhsT=lstm_sb[:, h * P : (h + 1) * P], rhs=ident_bf16[:], start=True, stop=True
-            )
+        lstm_cols = lstm_sb[:].rearrange("b (p e) -> b e p", e=2)
+        for e in range(2):
+            nc.tensor.matmul(out=comb_ps[0][:, e, :], lhsT=lstm_cols[:, e, :], rhs=ident_bf16[:], start=True, stop=True)
         comb_grouped = [
             keep.tile([P, B, PACK], BF16, align_bytes=64, name="comb_grouped%d" % g)
             for g in range(COMBINE_PASSES)
@@ -131,17 +136,14 @@ def tile_tkancell_pa_s_kernel(
             for g in range(COMBINE_PASSES)
         ]
 
-        def regroup_base(copy, l, lo=0, hi=U):
-            regroup(copy, layer_grouped[l][:, 0, :, :], base_raw[l][:], lo, hi)
+        def regroup_base(copy, l):
+            regroup_kan(copy, layer_grouped[l][:, 0, :, :], base_raw[l][:])
 
         def regroup_spline(copy, l, c):
-            regroup(copy, layer_grouped[l][:, 1 + c, :, :], spline_raw[l][c])
+            regroup_kan(copy, layer_grouped[l][:, 1 + c, :, :], spline_raw[l][c])
 
         def regroup_combine(copy, g):
             regroup(copy, combine_grouped[g][:], combine_raw[g][:])
-
-        regroup_base(on_vector, 0, 0, BASE0_VECTOR_COLS)
-        regroup_base(on_scalar, 0, BASE0_VECTOR_COLS, U)
 
         silu_grouped = keep.tile([P, B, PACK], BF16, align_bytes=64)
         nc.scalar.activation(
@@ -186,37 +188,39 @@ def tile_tkancell_pa_s_kernel(
         def comb_copy(g):
             nc.scalar.copy(out=comb_grouped[g][:], in_=comb_ps[g][:].rearrange("p t b -> p b t"))
 
+        regroup_base(on_vector, 0)
         regroup_spline(on_vector, 0, 0)
         base0 = quantise_slots(0, 0, 1, "base0")
         regroup_spline(on_vector, 0, 1)
         spline0a = quantise_slots(0, 1, 2, "spline0a")
         regroup_base(on_vector, 1)
-        silu = quantise(silu_grouped[:].rearrange("p b j -> p (b j)"), B, "silu")
         spline0b = quantise_slots(0, 2, 3, "spline0b")
-        base1 = quantise_slots(1, 0, 1, "base1")
+        silu = quantise(silu_grouped[:].rearrange("p b j -> p (b j)"), B, "silu")
         regroup_spline(on_scalar, 1, 0)
         regroup_spline(on_scalar, 1, 1)
         regroup_base(on_vector, 2)
         bases = quantise(bases_grouped[:].rearrange("p c b j -> p (c b j)"), NB * B, "bases")
         acts = [(silu, 0), (bases, 0), (bases, B)]
         layer_matmuls(0, [(base0, 0), (spline0a, 0), (spline0b, 0)])
+        base1 = quantise_slots(1, 0, 1, "base1")
+        spline1a = quantise_slots(1, 1, 2, "spline1a")
         regroup_spline(on_vector, 2, 0)
         regroup_spline(on_scalar, 2, 1)
-        spline1 = quantise_slots(1, 1, 3, "spline1")
-        layer_matmuls(1, [(base1, 0), (spline1, 0), (spline1, U)])
+        spline1b = quantise_slots(1, 2, 3, "spline1b")
+        layer_matmuls(1, [(base1, 0), (spline1a, 0), (spline1b, 0)])
         comb_copy(0)
         base2 = quantise_slots(2, 0, 2, "base2")
         spline2 = quantise_slots(2, 2, 3, "spline2")
         layer_matmuls(2, [(base2, 0), (base2, U), (spline2, 0)])
-        regroup_combine(on_vector, 0)
-        regroup_combine(on_scalar, 1)
-        comb_copy(1)
+        regroup_combine(on_scalar, 0)
+        regroup_combine(on_vector, 1)
         comb0 = quantise(comb_grouped[0][:].rearrange("p b j -> p (b j)"), B, "comb0")
         combine0 = quantise(combine_grouped[0][:].rearrange("p w j -> p (w j)"), U, "combine0")
-        out_ps = psum.tile([B, U], F32)
-        mx_pass(out_ps[:], comb0, slice(0, B), combine0, slice(0, U), True, False)
+        comb_copy(1)
         combine1 = quantise(combine_grouped[1][:].rearrange("p w j -> p (w j)"), U, "combine1")
         comb1 = quantise(comb_grouped[1][:].rearrange("p b j -> p (b j)"), B, "comb1")
+        out_ps = psum.tile([B, U], F32)
+        mx_pass(out_ps[:], comb0, slice(0, B), combine0, slice(0, U), True, False)
         mx_pass(out_ps[:], comb1, slice(0, B), combine1, slice(0, U), False, True)
         out_sb = keep.tile([B, U], F32)
         nc.vector.tensor_tensor(out=out_sb[:], in0=out_ps[:], in1=bias_all[:], op=ALU.add)

@@ -89,10 +89,10 @@ def tile_tkancell_pa_s_kernel(
         bias_all = keep.tile([P, U], BF16)
         nc.sync.dma_start(out=bias_all[:], in_=combine_b.partition_broadcast(P))
 
-        def regroup(copy, grouped, raw):
+        def regroup(copy, grouped, raw, lo=0, hi=U):
             copy(
-                out=grouped.rearrange("p (c i) j -> p c j i", i=4),
-                in_=raw.rearrange("p j (c i) -> p c j i", i=4),
+                out=grouped[:, lo:hi, :].rearrange("p (c i) j -> p c j i", i=4),
+                in_=raw[:, :, lo:hi].rearrange("p j (c i) -> p c j i", i=4),
             )
 
         def regroup_kan(copy, grouped, raw):
@@ -142,8 +142,8 @@ def tile_tkancell_pa_s_kernel(
         def regroup_spline(copy, l, c):
             regroup_kan(copy, layer_grouped[l][:, 1 + c, :, :], spline_raw[l][c])
 
-        def regroup_combine(copy, g):
-            regroup(copy, combine_grouped[g][:], combine_raw[g][:])
+        def regroup_combine(copy, g, lo=0, hi=U):
+            regroup(copy, combine_grouped[g][:], combine_raw[g][:], lo, hi)
 
         silu_grouped = keep.tile([P, B, PACK], BF16, align_bytes=64)
         nc.scalar.activation(
@@ -212,16 +212,21 @@ def tile_tkancell_pa_s_kernel(
         base2 = quantise_slots(2, 0, 2, "base2")
         spline2 = quantise_slots(2, 2, 3, "spline2")
         layer_matmuls(2, [(base2, 0), (base2, U), (spline2, 0)])
-        regroup_combine(on_scalar, 0)
+        regroup_combine(on_scalar, 0, U // 2, U)
+        regroup_combine(on_vector, 0, 0, U // 2)
         regroup_combine(on_vector, 1)
         comb0 = quantise(comb_grouped[0][:].rearrange("p b j -> p (b j)"), B, "comb0")
         combine0 = quantise(combine_grouped[0][:].rearrange("p w j -> p (w j)"), U, "combine0")
         comb_copy(1)
         combine1 = quantise(combine_grouped[1][:].rearrange("p w j -> p (w j)"), U, "combine1")
         comb1 = quantise(comb_grouped[1][:].rearrange("p b j -> p (b j)"), B, "comb1")
-        out_ps = psum.tile([B, U], F32)
-        mx_pass(out_ps[:], comb0, slice(0, B), combine0, slice(0, U), True, False)
-        mx_pass(out_ps[:], comb1, slice(0, B), combine1, slice(0, U), False, True)
-        out_sb = keep.tile([B, U], F32)
-        nc.vector.tensor_tensor(out=out_sb[:], in0=out_ps[:], in1=bias_all[:], op=ALU.add)
-        nc.sync.dma_start(out=out, in_=out_sb[:])
+        halves = [slice(h * P, (h + 1) * P) for h in range(HALVES)]
+        out_ps = [psum.tile([B, P], F32, name="out_ps%d" % h) for h in range(HALVES)]
+        for h in range(HALVES):
+            mx_pass(out_ps[h][:], comb0, slice(0, B), combine0, halves[h], True, False)
+        for h in range(HALVES):
+            mx_pass(out_ps[h][:], comb1, slice(0, B), combine1, halves[h], False, True)
+        for h in range(HALVES):
+            out_sb = keep.tile([B, P], F32, name="out_sb%d" % h)
+            nc.vector.tensor_tensor(out=out_sb[:], in0=out_ps[h][:], in1=bias_all[:, halves[h]], op=ALU.add)
+            (nc.sync if h == 0 else nc.scalar).dma_start(out=out[:, halves[h]], in_=out_sb[:])

@@ -220,13 +220,9 @@ def tile_tkancell_pa_s_kernel(
         comb_copy(1)
         combine1 = quantise(combine_grouped[1][:].rearrange("p w j -> p (w j)"), U, "combine1")
         comb1 = quantise(comb_grouped[1][:].rearrange("p b j -> p (b j)"), B, "comb1")
-        halves = [slice(h * P, (h + 1) * P) for h in range(HALVES)]
-        out_ps = [psum.tile([B, P], F32, name="out_ps%d" % h) for h in range(HALVES)]
-        for h in range(HALVES):
-            mx_pass(out_ps[h][:], comb0, slice(0, B), combine0, halves[h], True, False)
-        for h in range(HALVES):
-            mx_pass(out_ps[h][:], comb1, slice(0, B), combine1, halves[h], False, True)
-        for h in range(HALVES):
-            out_sb = keep.tile([B, P], F32, name="out_sb%d" % h)
-            nc.vector.tensor_tensor(out=out_sb[:], in0=out_ps[h][:], in1=bias_all[:, halves[h]], op=ALU.add)
-            (nc.sync if h == 0 else nc.scalar).dma_start(out=out[:, halves[h]], in_=out_sb[:])
+        out_ps = psum.tile([B, U], F32)
+        mx_pass(out_ps[:], comb0, slice(0, B), combine0, slice(0, U), True, False)
+        mx_pass(out_ps[:], comb1, slice(0, B), combine1, slice(0, U), False, True)
+        out_sb = keep.tile([B, U], F32)
+        nc.vector.tensor_tensor(out=out_sb[:], in0=out_ps[:], in1=bias_all[:], op=ALU.add)
+        nc.sync.dma_start(out=out, in_=out_sb[:])

@@ -57,10 +57,16 @@ def tile_tkancell_pa_s_kernel(
         silu_one = keep.tile([P, 1], F32)
         nc.scalar.activation(out=silu_one[:], in_=one[:], func=ACT.Silu)
 
+        ones = keep.tile([P, P], BF16)
+        nc.vector.memset(ones[:], 1.0)
+        bias_rows = keep.tile([P, U], BF16)
+        nc.vector.memset(bias_rows[:], 0.0)
+
         base_raw = []
         spline_raw = []
         x_sb = keep.tile([B, D], BF16)
         nc.sync.dma_start(out=x_sb[:], in_=x)
+        nc.sync.dma_start(out=bias_rows[0:1, :], in_=combine_b.rearrange("(o n) -> o n", o=1))
         for l in range(L):
             raw = keep.tile([P, PACK, U], BF16, name="base_raw%d" % l)
             nc.sync.dma_start(out=raw[:], in_=kan_base_w[l].rearrange("(p j) w -> p j w", j=PACK))
@@ -86,8 +92,6 @@ def tile_tkancell_pa_s_kernel(
                 in_=combine_w.rearrange("(g s p e) n -> g p s e n", g=COMBINE_PASSES, s=2, e=2)[g],
             )
             combine_raw.append(raw)
-        bias_all = keep.tile([P, U], BF16)
-        nc.sync.dma_start(out=bias_all[:], in_=combine_b.partition_broadcast(P))
 
         def regroup(copy, grouped, raw, lo=0, hi=U):
             copy(
@@ -117,6 +121,10 @@ def tile_tkancell_pa_s_kernel(
         for c in range(2):
             nc.tensor.transpose(xt_ps[:, c, :], x_words[:, c, :], ident_f32[:])
         xt = xt_ps[:].rearrange("p c b -> p (c b)").bitcast(BF16)
+
+        bias_ps = psum.tile([P, U], BF16)
+        nc.tensor.matmul(out=bias_ps[:], lhsT=ones[:], rhs=bias_rows[:], start=True, stop=True)
+        bias_all = keep.tile([P, U], BF16)
 
         comb_ps = [psum.tile([P, PACK, B], F32, name="comb_ps%d" % g) for g in range(COMBINE_PASSES)]
         lstm_cols = lstm_sb[:].rearrange("b (p e) -> b e p", e=2)
@@ -151,6 +159,7 @@ def tile_tkancell_pa_s_kernel(
             in_=xt.rearrange("p (c b e) -> p b c e", c=2, e=2),
             func=ACT.Silu,
         )
+        nc.scalar.copy(out=bias_all[:], in_=bias_ps[:])
         half_dist = keep.tile([P, NB, 2 * 2 * B], F32)
         for k in range(NB):
             nc.scalar.activation(

@@ -22,6 +22,8 @@ C = (1 + L) * U
 HALVES = U // P
 LAYER_PASSES = 1 + NB
 COMBINE_PASSES = C // (P * PACK)
+LAST_VECTOR_M = 48
+COMBINE0_VECTOR_COLS = 64
 
 FLOPS = 2 * B * (L * D * U + L * D * NB * U + C * U)
 
@@ -66,7 +68,6 @@ def tile_tkancell_pa_s_kernel(
         spline_raw = []
         x_sb = keep.tile([B, D], BF16)
         nc.sync.dma_start(out=x_sb[:], in_=x)
-        nc.sync.dma_start(out=bias_rows[0:1, :], in_=combine_b.rearrange("(o n) -> o n", o=1))
         for l in range(L):
             raw = keep.tile([P, PACK, U], BF16, name="base_raw%d" % l)
             nc.sync.dma_start(out=raw[:], in_=kan_base_w[l].rearrange("(p j) w -> p j w", j=PACK))
@@ -76,6 +77,7 @@ def tile_tkancell_pa_s_kernel(
                 halves = [keep.tile([P, PACK, U], BF16, name="spline_raw0_%d" % c) for c in range(NB)]
                 for c in range(NB):
                     nc.sync.dma_start(out=halves[c][:], in_=rows[:, c, :, :])
+                nc.sync.dma_start(out=bias_rows[0:1, :], in_=combine_b.rearrange("(o n) -> o n", o=1))
                 spline_raw.append([half[:] for half in halves])
             else:
                 raw = keep.tile([P, NB, PACK, U], BF16, name="spline_raw%d" % l)
@@ -99,10 +101,12 @@ def tile_tkancell_pa_s_kernel(
                 in_=raw[:, :, lo:hi].rearrange("p j (c i) -> p c j i", i=4),
             )
 
-        def regroup_kan(copy, grouped, raw):
+        def regroup_kan(copy, grouped, raw, lo=0, hi=P):
             copy(
-                out=grouped.rearrange("p (e c a) j -> p c j a e", e=2, a=2),
-                in_=raw.rearrange("p j (c a e) -> p c j a e", a=2, e=2),
+                out=grouped.rearrange("p (e m) j -> p e m j", e=2)[:, :, lo:hi, :].rearrange(
+                    "p e (c a) j -> p c j a e", a=2
+                ),
+                in_=raw[:, :, 2 * lo : 2 * hi].rearrange("p j (c a e) -> p c j a e", a=2, e=2),
             )
 
         on_vector = nc.vector.tensor_copy
@@ -116,11 +120,19 @@ def tile_tkancell_pa_s_kernel(
         nc.vector.memset(knot_shift[:, 0:1], 0.5)
         nc.vector.memset(knot_shift[:, 1:2], -0.5)
 
-        xt_ps = psum.tile([P, 2, B], F32)
-        x_words = x_sb[:].bitcast(F32).rearrange("b (p c) -> b c p", c=2)
-        for c in range(2):
-            nc.tensor.transpose(xt_ps[:, c, :], x_words[:, c, :], ident_f32[:])
+        silu_sb = keep.tile([B, D], BF16)
+        nc.scalar.activation(out=silu_sb[:], in_=x_sb[:], func=ACT.Silu)
+
+        def transpose_words(name, rows):
+            words_ps = psum.tile([P, 2, B], F32, name=name)
+            words = rows[:].bitcast(F32).rearrange("b (p c) -> b c p", c=2)
+            for c in range(2):
+                nc.tensor.transpose(words_ps[:, c, :], words[:, c, :], ident_f32[:])
+            return words_ps
+
+        xt_ps = transpose_words("xt_ps", x_sb)
         xt = xt_ps[:].rearrange("p c b -> p (c b)").bitcast(BF16)
+        silu_ps = transpose_words("silu_ps", silu_sb)
 
         bias_ps = psum.tile([P, U], BF16)
         nc.tensor.matmul(out=bias_ps[:], lhsT=ones[:], rhs=bias_rows[:], start=True, stop=True)
@@ -135,36 +147,33 @@ def tile_tkancell_pa_s_kernel(
             for g in range(COMBINE_PASSES)
         ]
 
-        layer_grouped = [
-            keep.tile([P, LAYER_PASSES, U, PACK], BF16, align_bytes=64, name="layer_grouped%d" % l)
-            for l in range(L)
-        ]
-        combine_grouped = [
-            keep.tile([P, U, PACK], BF16, align_bytes=64, name="combine_grouped%d" % g)
-            for g in range(COMBINE_PASSES)
-        ]
+        slots = ["base0", "spline0a", "spline0b", "base1", "spline1a", "spline1b", "base2", "spline2a", "spline2b"]
+        slots += ["combine0", "combine1"]
+        grouped_all = keep.tile([P, len(slots), U, PACK], BF16, align_bytes=64)
+
+        def grouped_slot(name):
+            return grouped_all[:, slots.index(name), :, :]
 
         def regroup_base(copy, l):
-            regroup_kan(copy, layer_grouped[l][:, 0, :, :], base_raw[l][:])
+            regroup_kan(copy, grouped_slot("base%d" % l), base_raw[l][:])
 
-        def regroup_spline(copy, l, c):
-            regroup_kan(copy, layer_grouped[l][:, 1 + c, :, :], spline_raw[l][c])
+        def regroup_spline(copy, l, c, lo=0, hi=P):
+            regroup_kan(copy, grouped_slot("spline%d%s" % (l, "ab"[c])), spline_raw[l][c], lo, hi)
 
         def regroup_combine(copy, g, lo=0, hi=U):
-            regroup(copy, combine_grouped[g][:], combine_raw[g][:], lo, hi)
+            regroup(copy, grouped_slot("combine%d" % g), combine_raw[g][:], lo, hi)
 
-        silu_grouped = keep.tile([P, B, PACK], BF16, align_bytes=64)
-        nc.scalar.activation(
-            out=silu_grouped[:].rearrange("p b (c e) -> p b c e", c=2),
-            in_=xt.rearrange("p (c b e) -> p b c e", c=2, e=2),
-            func=ACT.Silu,
-        )
-        nc.scalar.copy(out=bias_all[:], in_=bias_ps[:])
         half_dist = keep.tile([P, NB, 2 * 2 * B], F32)
         for k in range(NB):
             nc.scalar.activation(
                 out=half_dist[:, k, :], in_=xt, func=ACT.Abs, scale=0.5, bias=knot_shift[:, k : k + 1]
             )
+        silu_grouped = keep.tile([P, B, PACK], BF16, align_bytes=64)
+        nc.scalar.copy(
+            out=silu_grouped[:].rearrange("p b j -> p (b j)").bitcast(F32).rearrange("p (b c) -> p b c", c=2),
+            in_=silu_ps[:].rearrange("p c b -> p b c"),
+        )
+        nc.scalar.copy(out=bias_all[:], in_=bias_ps[:])
         bases_grouped = keep.tile([P, NB, B, PACK], BF16, align_bytes=64)
         nc.scalar.activation(
             out=bases_grouped[:].rearrange("p c b (e k) -> p (c b e) k", k=NB),
@@ -174,15 +183,21 @@ def tile_tkancell_pa_s_kernel(
             bias=one[:],
         )
 
-        def quantise_slots(l, lo, hi, name):
-            return quantise(layer_grouped[l][:, lo:hi, :, :].rearrange("p s w j -> p (s w j)"), (hi - lo) * U, name)
+        weights = {}
 
-        def layer_matmuls(l, weights):
+        def quantise_slots(*names):
+            lo = slots.index(names[0])
+            grouped = grouped_all[:, lo : lo + len(names), :, :].rearrange("p s w j -> p (s w j)")
+            pair = quantise(grouped, len(names) * U, names[0])
+            for i, name in enumerate(names):
+                weights[name] = (pair, i * U)
+
+        def layer_matmuls(l):
             for h in range(HALVES):
                 t = (1 + l) * HALVES + h
                 acc = comb_ps[t // PACK][:, t % PACK, :]
-                for c in range(LAYER_PASSES):
-                    pair, first = weights[c]
+                for c, name in enumerate(["base%d" % l, "spline%da" % l, "spline%db" % l]):
+                    pair, first = weights[name]
                     act, act_first = acts[c]
                     mx_pass(
                         acc,
@@ -199,39 +214,41 @@ def tile_tkancell_pa_s_kernel(
 
         regroup_base(on_vector, 0)
         regroup_spline(on_vector, 0, 0)
-        base0 = quantise_slots(0, 0, 1, "base0")
         regroup_spline(on_vector, 0, 1)
-        spline0a = quantise_slots(0, 1, 2, "spline0a")
+        quantise_slots("base0", "spline0a")
         regroup_base(on_vector, 1)
-        spline0b = quantise_slots(0, 2, 3, "spline0b")
         silu = quantise(silu_grouped[:].rearrange("p b j -> p (b j)"), B, "silu")
+        quantise_slots("spline0b", "base1")
         regroup_spline(on_scalar, 1, 0)
         regroup_spline(on_scalar, 1, 1)
         regroup_base(on_vector, 2)
         bases = quantise(bases_grouped[:].rearrange("p c b j -> p (c b j)"), NB * B, "bases")
         acts = [(silu, 0), (bases, 0), (bases, B)]
-        layer_matmuls(0, [(base0, 0), (spline0a, 0), (spline0b, 0)])
-        base1 = quantise_slots(1, 0, 1, "base1")
-        spline1a = quantise_slots(1, 1, 2, "spline1a")
+        layer_matmuls(0)
+        quantise_slots("spline1a")
         regroup_spline(on_vector, 2, 0)
-        regroup_spline(on_scalar, 2, 1)
-        spline1b = quantise_slots(1, 2, 3, "spline1b")
-        layer_matmuls(1, [(base1, 0), (spline1a, 0), (spline1b, 0)])
+        regroup_spline(on_scalar, 2, 1, LAST_VECTOR_M, P)
+        quantise_slots("spline1b")
+        layer_matmuls(1)
+        regroup_spline(on_vector, 2, 1, 0, LAST_VECTOR_M)
         comb_copy(0)
-        base2 = quantise_slots(2, 0, 2, "base2")
-        spline2 = quantise_slots(2, 2, 3, "spline2")
-        layer_matmuls(2, [(base2, 0), (base2, U), (spline2, 0)])
-        regroup_combine(on_scalar, 0, U // 2, U)
-        regroup_combine(on_vector, 0, 0, U // 2)
+        quantise_slots("base2", "spline2a")
+        quantise_slots("spline2b")
+        layer_matmuls(2)
+        regroup_combine(on_scalar, 0, COMBINE0_VECTOR_COLS, U)
+        regroup_combine(on_vector, 0, 0, COMBINE0_VECTOR_COLS)
         regroup_combine(on_vector, 1)
         comb0 = quantise(comb_grouped[0][:].rearrange("p b j -> p (b j)"), B, "comb0")
-        combine0 = quantise(combine_grouped[0][:].rearrange("p w j -> p (w j)"), U, "combine0")
+        quantise_slots("combine0")
         comb_copy(1)
-        combine1 = quantise(combine_grouped[1][:].rearrange("p w j -> p (w j)"), U, "combine1")
+        quantise_slots("combine1")
         comb1 = quantise(comb_grouped[1][:].rearrange("p b j -> p (b j)"), B, "comb1")
         out_ps = psum.tile([B, U], F32)
-        mx_pass(out_ps[:], comb0, slice(0, B), combine0, slice(0, U), True, False)
-        mx_pass(out_ps[:], comb1, slice(0, B), combine1, slice(0, U), False, True)
+        for g, comb in enumerate([comb0, comb1]):
+            pair, first = weights["combine%d" % g]
+            mx_pass(
+                out_ps[:], comb, slice(0, B), pair, slice(first, first + U), g == 0, g == COMBINE_PASSES - 1
+            )
         out_sb = keep.tile([B, U], F32)
         nc.vector.tensor_tensor(out=out_sb[:], in0=out_ps[:], in1=bias_all[:], op=ALU.add)
         nc.sync.dma_start(out=out, in_=out_sb[:])

from contextlib import ExitStack

import concourse.mybir as mybir
from concourse.masks import make_identity

F32 = mybir.dt.float32
BF16 = mybir.dt.bfloat16
U32 = mybir.dt.uint32
U8 = mybir.dt.uint8
FP8X4 = mybir.dt.float8_e4m3fn_x4
ACT = mybir.ActivationFunctionType
ALU = mybir.AluOpType

P = 128
PACK = 4
B = 128
D = 512
U = 256
L = 3
NB = 2
C = (1 + L) * U
HALVES = U // P
LAYER_PASSES = 1 + NB
COMBINE_PASSES = C // (P * PACK)
LAST_VECTOR_M = 48
COMBINE0_VECTOR_COLS = 64

FLOPS = 2 * B * (L * D * U + L * D * NB * U + C * U)


def tile_tkancell_pa_s_kernel(
    tc, x, lstm_out, kan_base_w, kan_spline_w, combine_w, combine_b, out
):
    nc = tc.nc
    with ExitStack() as ctx:
        keep = ctx.enter_context(tc.tile_pool(name="keep", bufs=1))
        psum = ctx.enter_context(tc.psum_pool(name="psum", bufs=1))
        ctx.enter_context(tc.manual_schedule())

        def quantise(grouped, width, name):
            codes = keep.tile([P, width], U32, align_bytes=64, name=name + "_codes")
            scales = keep.tile([P, width], U8, align_bytes=64, name=name + "_scales")
            nc.vector.quantize_mx(out=codes[:].bitcast(FP8X4), scales=scales[:], in_=grouped)
            return codes, scales

        def mx_pass(acc, stationary, cols, moving, moving_cols, start, stop):
            nc.tensor.matmul_mx(
                out=acc,
                lhsT=stationary[0][:, cols].bitcast(FP8X4),
                lhsT_scale=stationary[1][:, cols],
                rhs=moving[0][:, moving_cols].bitcast(FP8X4),
                rhs_scale=moving[1][:, moving_cols],
                start=start,
                stop=stop,
            )

        one = keep.tile([P, 1], F32)
        nc.vector.memset(one[:], 1.0)
        silu_one = keep.tile([P, 1], F32)
        nc.scalar.activation(out=silu_one[:], in_=one[:], func=ACT.Silu)

        ones = keep.tile([P, P], BF16)
        nc.vector.memset(ones[:], 1.0)
        bias_rows = keep.tile([P, U], BF16)
        nc.vector.memset(bias_rows[:], 0.0)

        base_raw = []
        spline_raw = []
        x_sb = keep.tile([B, D], BF16)
        nc.sync.dma_start(out=x_sb[:], in_=x)
        for l in range(L):
            raw = keep.tile([P, PACK, U], BF16, name="base_raw%d" % l)
            nc.sync.dma_start(out=raw[:], in_=kan_base_w[l].rearrange("(p j) w -> p j w", j=PACK))
            base_raw.append(raw)
            rows = kan_spline_w[l].rearrange("(p c j) w -> p c j w", c=NB, j=PACK)
            if l == 0:
                halves = [keep.tile([P, PACK, U], BF16, name="spline_raw0_%d" % c) for c in range(NB)]
                for c in range(NB):
                    nc.sync.dma_start(out=halves[c][:], in_=rows[:, c, :, :])
                nc.sync.dma_start(out=bias_rows[0:1, :], in_=combine_b.rearrange("(o n) -> o n", o=1))
                spline_raw.append([half[:] for half in halves])
            else:
                raw = keep.tile([P, NB, PACK, U], BF16, name="spline_raw%d" % l)
                nc.sync.dma_start(out=raw[:], in_=rows)
                spline_raw.append([raw[:, c, :, :] for c in range(NB)])
            if l == 1:
                lstm_sb = keep.tile([B, U], BF16)
                nc.sync.dma_start(out=lstm_sb[:], in_=lstm_out)
        combine_raw = []
        for g in range(COMBINE_PASSES):
            raw = keep.tile([P, PACK, U], BF16, name="combine_raw%d" % g)
            nc.sync.dma_start(
                out=raw[:].rearrange("p (s e) n -> p s e n", s=2),
                in_=combine_w.rearrange("(g s p e) n -> g p s e n", g=COMBINE_PASSES, s=2, e=2)[g],
            )
            combine_raw.append(raw)

        def regroup(copy, grouped, raw, lo=0, hi=U):
            copy(
                out=grouped[:, lo:hi, :].rearrange("p (c i) j -> p c j i", i=4),
                in_=raw[:, :, lo:hi].rearrange("p j (c i) -> p c j i", i=4),
            )

        def regroup_kan(copy, grouped, raw, lo=0, hi=P):
            copy(
                out=grouped.rearrange("p (e m) j -> p e m j", e=2)[:, :, lo:hi, :].rearrange(
                    "p e (c a) j -> p c j a e", a=2
                ),
                in_=raw[:, :, 2 * lo : 2 * hi].rearrange("p j (c a e) -> p c j a e", a=2, e=2),
            )

        on_vector = nc.vector.tensor_copy
        on_scalar = nc.scalar.copy

        ident_f32 = keep.tile([P, P], F32)
        make_identity(nc, ident_f32[:])
        ident_bf16 = keep.tile([P, P], BF16)
        make_identity(nc, ident_bf16[:])
        knot_shift = keep.tile([P, NB], F32)
        nc.vector.memset(knot_shift[:, 0:1], 0.5)
        nc.vector.memset(knot_shift[:, 1:2], -0.5)

        silu_sb = keep.tile([B, D], BF16)
        nc.scalar.activation(out=silu_sb[:], in_=x_sb[:], func=ACT.Silu)

        def transpose_words(name, rows):
            words_ps = psum.tile([P, 2, B], F32, name=name)
            words = rows[:].bitcast(F32).rearrange("b (p c) -> b c p", c=2)
            for c in range(2):
                nc.tensor.transpose(words_ps[:, c, :], words[:, c, :], ident_f32[:])
            return words_ps

        xt_ps = transpose_words("xt_ps", x_sb)
        xt = xt_ps[:].rearrange("p c b -> p (c b)").bitcast(BF16)
        silu_ps = transpose_words("silu_ps", silu_sb)

        bias_ps = psum.tile([P, U], BF16)
        nc.tensor.matmul(out=bias_ps[:], lhsT=ones[:], rhs=bias_rows[:], start=True, stop=True)
        bias_all = keep.tile([P, U], BF16)

        comb_ps = [psum.tile([P, PACK, B], F32, name="comb_ps%d" % g) for g in range(COMBINE_PASSES)]
        lstm_cols = lstm_sb[:].rearrange("b (p e) -> b e p", e=2)
        for e in range(2):
            nc.tensor.matmul(out=comb_ps[0][:, e, :], lhsT=lstm_cols[:, e, :], rhs=ident_bf16[:], start=True, stop=True)
        comb_grouped = [
            keep.tile([P, B, PACK], BF16, align_bytes=64, name="comb_grouped%d" % g)
            for g in range(COMBINE_PASSES)
        ]

        slots = ["base0", "spline0a", "spline0b", "base1", "spline1a", "spline1b", "base2", "spline2a", "spline2b"]
        slots += ["combine0", "combine1"]
        grouped_all = keep.tile([P, len(slots), U, PACK], BF16, align_bytes=64)

        def grouped_slot(name):
            return grouped_all[:, slots.index(name), :, :]

        def regroup_base(copy, l):
            regroup_kan(copy, grouped_slot("base%d" % l), base_raw[l][:])

        def regroup_spline(copy, l, c, lo=0, hi=P):
            regroup_kan(copy, grouped_slot("spline%d%s" % (l, "ab"[c])), spline_raw[l][c], lo, hi)

        def regroup_combine(copy, g, lo=0, hi=U):
            regroup(copy, grouped_slot("combine%d" % g), combine_raw[g][:], lo, hi)

        half_dist = keep.tile([P, NB, 2 * 2 * B], F32)
        for k in range(NB):
            nc.scalar.activation(
                out=half_dist[:, k, :], in_=xt, func=ACT.Abs, scale=0.5, bias=knot_shift[:, k : k + 1]
            )
        silu_grouped = keep.tile([P, B, PACK], BF16, align_bytes=64)
        nc.scalar.copy(
            out=silu_grouped[:].rearrange("p b j -> p (b j)").bitcast(F32).rearrange("p (b c) -> p b c", c=2),
            in_=silu_ps[:].rearrange("p c b -> p b c"),
        )
        nc.scalar.copy(out=bias_all[:], in_=bias_ps[:])
        bases_grouped = keep.tile([P, NB, B, PACK], BF16, align_bytes=64)
        nc.scalar.activation(
            out=bases_grouped[:].rearrange("p c b (e k) -> p (c b e) k", k=NB),
            in_=half_dist[:].rearrange("p k n -> p n k"),
            func=ACT.Relu,
            scale=-1.0,
            bias=one[:],
        )

        weights = {}

        def quantise_slots(*names):
            lo = slots.index(names[0])
            grouped = grouped_all[:, lo : lo + len(names), :, :].rearrange("p s w j -> p (s w j)")
            pair = quantise(grouped, len(names) * U, names[0])
            for i, name in enumerate(names):
                weights[name] = (pair, i * U)

        def layer_matmuls(l):
            for h in range(HALVES):
                t = (1 + l) * HALVES + h
                acc = comb_ps[t // PACK][:, t % PACK, :]
                for c, name in enumerate(["base%d" % l, "spline%da" % l, "spline%db" % l]):
                    pair, first = weights[name]
                    act, act_first = acts[c]
                    mx_pass(
                        acc,
                        pair,
                        slice(first + h * P, first + (h + 1) * P),
                        act,
                        slice(act_first, act_first + B),
                        c == 0,
                        c == NB,
                    )

        def comb_copy(g):
            nc.scalar.copy(out=comb_grouped[g][:], in_=comb_ps[g][:].rearrange("p t b -> p b t"))

        regroup_base(on_vector, 0)
        regroup_spline(on_vector, 0, 0)
        regroup_spline(on_vector, 0, 1)
        quantise_slots("base0", "spline0a")
        regroup_base(on_vector, 1)
        silu = quantise(silu_grouped[:].rearrange("p b j -> p (b j)"), B, "silu")
        quantise_slots("spline0b", "base1")
        regroup_spline(on_scalar, 1, 0)
        regroup_spline(on_scalar, 1, 1)
        regroup_base(on_vector, 2)
        bases = quantise(bases_grouped[:].rearrange("p c b j -> p (c b j)"), NB * B, "bases")
        acts = [(silu, 0), (bases, 0), (bases, B)]
        layer_matmuls(0)
        quantise_slots("spline1a")
        regroup_spline(on_vector, 2, 0)
        regroup_spline(on_scalar, 2, 1, LAST_VECTOR_M, P)
        quantise_slots("spline1b")
        layer_matmuls(1)
        regroup_spline(on_vector, 2, 1, 0, LAST_VECTOR_M)
        comb_copy(0)
        quantise_slots("base2", "spline2a")
        quantise_slots("spline2b")
        layer_matmuls(2)
        regroup_combine(on_scalar, 0, COMBINE0_VECTOR_COLS, U)
        regroup_combine(on_vector, 0, 0, COMBINE0_VECTOR_COLS)
        regroup_combine(on_vector, 1)
        comb0 = quantise(comb_grouped[0][:].rearrange("p b j -> p (b j)"), B, "comb0")
        quantise_slots("combine0")
        comb_copy(1)
        quantise_slots("combine1")
        comb1 = quantise(comb_grouped[1][:].rearrange("p b j -> p (b j)"), B, "comb1")
        out_ps = psum.tile([B, U], F32)
        for g, comb in enumerate([comb0, comb1]):
            pair, first = weights["combine%d" % g]
            mx_pass(
                out_ps[:], comb, slice(0, B), pair, slice(first, first + U), g == 0, g == COMBINE_PASSES - 1
            )
        out_sb = keep.tile([B, U], F32)
        nc.vector.tensor_tensor(out=out_sb[:], in0=out_ps[:], in1=bias_all[:], op=ALU.add)
        nc.sync.dma_start(out=out, in_=out_sb[:])
